import numpy as np
import ml_dtypes


def mxq(x, axis, fmt="e4m3"):
    dtype, down = {"e4m3": (ml_dtypes.float8_e4m3fn, 7), "e5m2": (ml_dtypes.float8_e5m2, 14)}[fmt]
    v = np.moveaxis(np.asarray(x, np.float32).astype(ml_dtypes.bfloat16).astype(np.float64), axis, -1)
    blocks = v.reshape(v.shape[:-1] + (-1, 32))
    amax = np.abs(blocks).max(-1, keepdims=True)
    byte = np.maximum(np.where(amax > 0, np.frexp(amax)[1] - 1 + 127, 0) - down, 1)
    scale = np.exp2(byte - 127.0)
    codes = (blocks / scale).astype(np.float32).astype(dtype).astype(np.float64)
    return np.moveaxis((codes * scale).reshape(v.shape), -1, axis)


WIDE = False


def mx_kscale(k):
    if not WIDE:
        return np.ones(k)
    levels = np.array([10, -10, 5, -5, 0])
    a = np.random.permutation(np.resize(levels, k // 512 * 4)).reshape(k // 512, 4)
    idx = np.arange(k)
    return np.exp2(a[idx // 512, idx % 128 // 32])


BF16 = ml_dtypes.bfloat16


def bf(x):
    return np.asarray(x, np.float32).astype(BF16)


def f64(x):
    return np.asarray(x).astype(np.float64)


E2M1 = np.array([0.0, 0.5, 1.0, 1.5, 2.0, 3.0, 4.0, 6.0, -0.0, -0.5, -1.0, -1.5, -2.0, -3.0, -4.0, -6.0])


def pack_weight(w, fmt):
    k, n = w.shape
    w = f64(bf(w)).reshape(k // 32, 32, n)
    amax = np.abs(w).max(1)
    if fmt == "e4m3":
        byte = np.frexp(amax)[1] - 1 + 127 - 7
    else:
        mant, ex = np.frexp(amax / 6.0)
        byte = np.where(mant > 0.5, ex, ex - 1) + 127
    byte = np.clip(np.where(amax > 0, byte, 1), 1, 254)
    scaled = (w * np.exp2(127.0 - byte)[:, None, :]).reshape(k, n).astype(np.float32)
    by_word = np.ascontiguousarray(scaled.reshape(k // 512, 128, 4, n).transpose(0, 1, 3, 2))
    if fmt == "e4m3":
        words = by_word.astype(ml_dtypes.float8_e4m3fn).view(np.uint8)
    else:
        c = by_word.astype(ml_dtypes.float4_e2m1fn).view(np.uint8) & 0xF
        words = c[..., 0::2] | (c[..., 1::2] << 4)
    return np.ascontiguousarray(words), np.ascontiguousarray(byte.astype(np.uint8).reshape(k // 512, 16, n))


def unpack_weight(words, scales, fmt):
    g, p, n, _ = words.shape
    if fmt == "e4m3":
        vals = np.ascontiguousarray(words).view(ml_dtypes.float8_e4m3fn).astype(np.float64)
    else:
        nib = np.empty((g, p, n, 4), np.uint8)
        nib[..., 0::2] = words & 0xF
        nib[..., 1::2] = words >> 4
        vals = E2M1[nib]
    vals = vals * np.repeat(np.exp2(scales.astype(np.float64) - 127.0), 8, axis=1)[..., None]
    return vals.transpose(0, 1, 3, 2).reshape(g * 512, n)

def pack4(w):
    words, scales = pack_weight(w, "e2m1")
    return words.reshape(words.shape[0], 128, -1), scales


def unpack4(words, scales):
    return unpack_weight(words.reshape(words.shape[0], 128, -1, 2), scales, "e2m1")


S, D, H, DH = 128, 16384, 16, 128
ROPE_BASE = 10000.0


def rotate_half(v):
    shp = v.shape
    p = v.reshape(*shp[:-1], shp[-1] // 2, 2)
    return np.stack((-p[..., 1], p[..., 0]), axis=-1).reshape(shp)


def rope_cos_sin(seq_len, dh):
    inv_freq = 1.0 / (ROPE_BASE ** (np.arange(0, dh, 2) / dh))
    t = np.arange(seq_len)
    freqs = t[:, None] * inv_freq[None, :]
    return np.repeat(np.cos(freqs), 2, axis=-1), np.repeat(np.sin(freqs), 2, axis=-1)


def setup_inputs():
    s = mx_kscale(D)
    x = bf(np.random.standard_normal((S, D)) * s)
    w = np.random.standard_normal((H * DH, D)) / np.sqrt(D) / s[None, :]
    words, scales = pack4(np.ascontiguousarray(w.T))
    return {"x": x, "w_words": words, "w_scales": scales}


def reference(x, w_words, w_scales):
    y = mxq(f64(x), 1, "e4m3") @ unpack4(w_words, w_scales)
    q = y.reshape(S, H, DH).transpose(1, 0, 2)
    cos, sin = rope_cos_sin(S, DH)
    return q * cos[None] + rotate_half(q) * sin[None]

@@ -1,0 +1,255 @@
+import math
+from contextlib import ExitStack
+
+import concourse.mybir as mybir
+from concourse.masks import make_identity
+
+F32 = mybir.dt.float32
+BF16 = mybir.dt.bfloat16
+I32 = mybir.dt.int32
+U32 = mybir.dt.uint32
+U8 = mybir.dt.uint8
+FP8X4 = mybir.dt.float8_e4m3fn_x4
+FP4X4 = mybir.dt.float4_e2m1fn_x4
+ALU = mybir.AluOpType
+ACT = mybir.ActivationFunctionType
+
+P = 128
+TOKENS = 128
+D_IN = 16384
+HEADS = 16
+HEAD_DIM = 128
+PAIRS = HEAD_DIM // 2
+D_OUT = HEADS * HEAD_DIM
+ROPE_BASE = 10000.0
+
+K_PASS = 4 * P
+PASSES = D_IN // K_PASS
+BANK_COLS = 512
+BANKS = D_OUT // BANK_COLS
+BANK_HEADS = BANK_COLS // HEAD_DIM
+FP4_BYTES = 2
+
+X_CHUNK_PASSES = 8
+X_CHUNKS = PASSES // X_CHUNK_PASSES
+X_CHUNK_COLS = X_CHUNK_PASSES * K_PASS
+PASS_WORDS = K_PASS // 2
+
+PHASE_PASSES = 8
+PHASES = PASSES // PHASE_PASSES
+W_LOAD_PASSES = 2
+W_LOAD_BYTES = W_LOAD_PASSES * D_OUT * FP4_BYTES
+PHASE_LOADS = PHASE_PASSES // W_LOAD_PASSES
+SCALE_DMA_PASSES = 4
+assert PHASE_PASSES * BANK_COLS * FP4_BYTES == W_LOAD_BYTES
+
+TWO_PI = 2.0 * math.pi
+TWO_PI_HIGH = 6.28125
+TWO_PI_MID = round((TWO_PI - TWO_PI_HIGH) * 2.0**25) / 2.0**25
+TWO_PI_LOW = TWO_PI - TWO_PI_HIGH - TWO_PI_MID
+ROUNDER = 1.5 * 2.0**23
+
+FLOPS = 2 * TOKENS * D_IN * D_OUT
+
+
+def tile_attention_pa_k_kernel(tc, x, w_words, w_scales, out):
+    nc = tc.nc
+    w_words_i32 = w_words.bitcast(I32)
+    w_scales_i32 = w_scales.bitcast(I32)
+
+    with ExitStack() as ctx:
+        consts = ctx.enter_context(tc.tile_pool(name="consts", bufs=1))
+        x_pool = ctx.enter_context(tc.tile_pool(name="x_raw", bufs=X_CHUNKS))
+        grouped_pool = ctx.enter_context(tc.tile_pool(name="grouped", bufs=2))
+        plane_pool = ctx.enter_context(tc.tile_pool(name="planes", bufs=1))
+        word_pool = ctx.enter_context(tc.tile_pool(name="words", bufs=2 * PHASE_LOADS))
+        rot_pool = ctx.enter_context(tc.tile_pool(name="rotation", bufs=2))
+        acc_pool = ctx.enter_context(tc.psum_pool(name="acc", bufs=1))
+        flip_pool = ctx.enter_context(tc.psum_pool(name="flipped", bufs=8 - BANKS))
+        ctx.enter_context(tc.manual_schedule())
+
+        x_raw = []
+        for c in range(X_CHUNKS):
+            chunk = x_pool.tile([P, X_CHUNK_COLS], BF16, name="x_raw")
+            nc.sync.dma_start(out=chunk[:], in_=x[:, c * X_CHUNK_COLS : (c + 1) * X_CHUNK_COLS])
+            x_raw.append(chunk)
+
+        ident = consts.tile([P, P], F32, name="ident")
+        make_identity(nc, ident[:])
+        position_i32 = consts.tile([P, 1], I32, name="position_i32")
+        nc.gpsimd.iota(position_i32[:], pattern=[[0, 1]], base=0, channel_multiplier=1)
+
+        planes = []
+        for i in range(2):
+            plane = plane_pool.tile([P, PHASE_PASSES * D_OUT], U8, name="planes%d" % i, align_bytes=64)
+            nc.vector.memset(plane[:].bitcast(I32), 0)
+            planes.append(plane)
+
+        def load_scales(phase):
+            plane_i32 = planes[phase % 2][:].bitcast(I32).rearrange("p (g n) -> p g n", g=PHASE_PASSES)
+            for first in range(0, PHASE_PASSES, SCALE_DMA_PASSES):
+                g0 = phase * PHASE_PASSES + first
+                for q in range(8):
+                    partition = 32 * (q // 4) + q % 4
+                    nc.sync.dma_start(
+                        out=plane_i32[partition : P : 64, first : first + SCALE_DMA_PASSES, :],
+                        in_=w_scales_i32[g0 : g0 + SCALE_DMA_PASSES, q : 16 : 8, :].rearrange("g q n -> q g n"),
+                    )
+
+        def load_words_by_pass(phase):
+            tiles = []
+            for i in range(PHASE_LOADS):
+                g0 = phase * PHASE_PASSES + i * W_LOAD_PASSES
+                words = word_pool.tile([P, W_LOAD_BYTES], U8, name="words", align_bytes=64)
+                nc.sync.dma_start(
+                    out=words[:].bitcast(I32).rearrange("p (g b) -> p g b", g=W_LOAD_PASSES),
+                    in_=w_words_i32[g0 : g0 + W_LOAD_PASSES].rearrange("g p b -> p g b"),
+                )
+                tiles.append(words)
+            return tiles
+
+        def load_words_by_bank(phase):
+            g0 = phase * PHASE_PASSES
+            bank_i32 = BANK_COLS * FP4_BYTES // 4
+            tiles = []
+            for j in range(BANKS):
+                words = word_pool.tile([P, W_LOAD_BYTES], U8, name="words", align_bytes=64)
+                nc.sync.dma_start(
+                    out=words[:].bitcast(I32).rearrange("p (g b) -> p g b", g=PHASE_PASSES),
+                    in_=w_words_i32[g0 : g0 + PHASE_PASSES, :, j * bank_i32 : (j + 1) * bank_i32].rearrange(
+                        "g p b -> p g b"
+                    ),
+                )
+                tiles.append(words)
+            return tiles
+
+        def load_phase(phase):
+            load_scales(phase)
+            if phase < PHASES - 1:
+                return load_words_by_pass(phase)
+            return load_words_by_bank(phase)
+
+        phase_words = {0: load_phase(0), 1: load_phase(1)}
+
+        x_codes = consts.tile([P, PASSES * TOKENS], U32, name="x_codes", align_bytes=64)
+        x_planes = consts.tile([P, PASSES * TOKENS], U8, name="x_planes", align_bytes=64)
+
+        def transpose_chunk(c):
+            words = x_raw[c][:].bitcast(F32)
+            grouped = grouped_pool.tile([P, X_CHUNK_COLS], BF16, name="grouped", align_bytes=64)
+            grouped_words = grouped[:].bitcast(F32).rearrange("p (g r u) -> p g r u", g=X_CHUNK_PASSES, u=2)
+            for b in range(X_CHUNK_PASSES // 2):
+                flipped = flip_pool.tile([P, 2, 2, TOKENS], F32, name="flipped")
+                for g in range(2):
+                    first = (2 * b + g) * PASS_WORDS
+                    for u in range(2):
+                        nc.tensor.transpose(flipped[:, g, u, :], words[:, first + u : first + PASS_WORDS : 2], ident[:])
+                copy = nc.vector.tensor_copy if b % 2 == 0 else nc.scalar.copy
+                copy(out=grouped_words[:, 2 * b : 2 * b + 2], in_=flipped[:].rearrange("p g u r -> p g r u"))
+            return grouped
+
+        def quantise_chunk(c, grouped):
+            cols = slice(c * X_CHUNK_PASSES * TOKENS, (c + 1) * X_CHUNK_PASSES * TOKENS)
+            nc.vector.quantize_mx(out=x_codes[:, cols].bitcast(FP8X4), scales=x_planes[:, cols], in_=grouped[:])
+
+        waiting = None
+        for c in range(X_CHUNKS):
+            grouped = transpose_chunk(c)
+            if waiting is not None:
+                quantise_chunk(c - 1, waiting)
+            waiting = grouped
+        quantise_chunk(X_CHUNKS - 1, waiting)
+
+        position = consts.tile([P, 1], F32, name="position")
+        nc.vector.tensor_copy(out=position[:], in_=position_i32[:])
+        frequency = consts.tile([P, PAIRS], F32, name="frequency")
+        nc.vector.memset(frequency[:, 0:1], 1.0)
+        m = 1
+        while m < PAIRS:
+            nc.vector.tensor_scalar(
+                out=frequency[:, m : 2 * m],
+                in0=frequency[:, 0:m],
+                scalar1=ROPE_BASE ** (-2.0 * m / HEAD_DIM),
+                scalar2=None,
+                op0=ALU.mult,
+            )
+            m *= 2
+        angle = consts.tile([P, 2, PAIRS], F32, name="angle")
+        nc.vector.tensor_scalar(
+            out=angle[:, 0, :], in0=frequency[:], scalar1=position[:, 0:1], scalar2=None, op0=ALU.mult
+        )
+        nc.vector.tensor_scalar(
+            out=angle[:, 1, :],
+            in0=frequency[:],
+            scalar1=position[:, 0:1],
+            scalar2=0.5 * math.pi,
+            op0=ALU.mult,
+            op1=ALU.add,
+        )
+        shifted = consts.tile([P, 2, PAIRS], F32, name="shifted")
+        nc.vector.tensor_scalar(
+            out=shifted[:], in0=angle[:], scalar1=1.0 / TWO_PI, scalar2=ROUNDER, op0=ALU.mult, op1=ALU.add
+        )
+        turns = consts.tile([P, 2, PAIRS], F32, name="turns")
+        nc.vector.tensor_scalar(out=turns[:], in0=shifted[:], scalar1=ROUNDER, scalar2=None, op0=ALU.subtract)
+        reduced = angle
+        for part, two_pi_part in enumerate((TWO_PI_HIGH, TWO_PI_MID, TWO_PI_LOW)):
+            less = consts.tile([P, 2, PAIRS], F32, name="reduced%d" % part)
+            nc.vector.scalar_tensor_tensor(
+                out=less[:], in0=turns[:], scalar=-two_pi_part, in1=reduced[:], op0=ALU.mult, op1=ALU.add
+            )
+            reduced = less
+        table = consts.tile([P, 2, PAIRS, 2], F32, name="table")
+        nc.scalar.activation(out=table[:, 0, :, 0], in_=reduced[:, 1, :], func=ACT.Sin)
+        nc.scalar.activation(out=table[:, 0, :, 1], in_=reduced[:, 0, :], func=ACT.Sin, scale=-1.0)
+        nc.scalar.activation(out=table[:, 1, :, 0], in_=reduced[:, 0, :], func=ACT.Sin)
+        nc.scalar.activation(out=table[:, 1, :, 1], in_=reduced[:, 1, :], func=ACT.Sin)
+        table_by_head = (
+            table[:].rearrange("p s q t -> p s (q t)").unsqueeze(2).to_broadcast([P, 2, BANK_HEADS, HEAD_DIM])
+        )
+
+        acc = [acc_pool.tile([P, BANK_COLS], F32, name="acc%d" % j) for j in range(BANKS)]
+
+        def multiply(g, j, words, first_byte):
+            plane_col = (g % PHASE_PASSES) * D_OUT + j * BANK_COLS
+            nc.tensor.matmul_mx(
+                out=acc[j][:],
+                lhsT=x_codes[:, g * TOKENS : (g + 1) * TOKENS].bitcast(FP8X4),
+                lhsT_scale=x_planes[:, g * TOKENS : (g + 1) * TOKENS],
+                rhs=words[:, first_byte : first_byte + BANK_COLS * FP4_BYTES].bitcast(FP4X4),
+                rhs_scale=planes[(g // PHASE_PASSES) % 2][:, plane_col : plane_col + BANK_COLS],
+                start=(g == 0),
+                stop=(g == PASSES - 1),
+            )
+
+        def rotate_and_store(j):
+            y = acc[j][:].rearrange("p (h d) -> p h d", h=BANK_HEADS).unsqueeze(1)
+            products = rot_pool.tile([P, 2, BANK_HEADS, HEAD_DIM], F32, name="products")
+            nc.vector.tensor_tensor(
+                out=products[:], in0=y.to_broadcast([P, 2, BANK_HEADS, HEAD_DIM]), in1=table_by_head, op=ALU.mult
+            )
+            terms = products[:].rearrange("p s h (q t) -> p h q s t", t=2)
+            rotated = rot_pool.tile([P, BANK_HEADS, PAIRS, 2], F32, name="rotated")
+            nc.vector.tensor_tensor(out=rotated[:], in0=terms[:, :, :, :, 0], in1=terms[:, :, :, :, 1], op=ALU.add)
+            nc.sync.dma_start(
+                out=out[j * BANK_HEADS : (j + 1) * BANK_HEADS].rearrange("h i d -> i h d"),
+                in_=rotated[:].rearrange("p h q s -> p h (q s)"),
+            )
+
+        for phase in range(PHASES - 1):
+            for i, words in enumerate(phase_words[phase]):
+                for g in range(W_LOAD_PASSES):
+                    for j in range(BANKS):
+                        multiply(
+                            phase * PHASE_PASSES + i * W_LOAD_PASSES + g,
+                            j,
+                            words,
+                            (g * D_OUT + j * BANK_COLS) * FP4_BYTES,
+                        )
+            if phase + 2 < PHASES:
+                phase_words[phase + 2] = load_phase(phase + 2)
+
+        for j, words in enumerate(phase_words[PHASES - 1]):
+            for g in range(PHASE_PASSES):
+                multiply((PHASES - 1) * PHASE_PASSES + g, j, words, g * BANK_COLS * FP4_BYTES)
+            rotate_and_store(j)

@@ -40,7 +40,6 @@ PHASES = PASSES // PHASE_PASSES
 W_LOAD_PASSES = 2
 W_LOAD_BYTES = W_LOAD_PASSES * D_OUT * FP4_BYTES
 PHASE_LOADS = PHASE_PASSES // W_LOAD_PASSES
-SCALE_DMA_PASSES = 4
 assert PHASE_PASSES * BANK_COLS * FP4_BYTES == W_LOAD_BYTES
 
 TWO_PI = 2.0 * math.pi
@@ -86,14 +85,14 @@ def tile_attention_pa_k_kernel(tc, x, w_words, w_scales, out):
             planes.append(plane)
 
         def load_scales(phase):
-            plane_i32 = planes[phase % 2][:].bitcast(I32).rearrange("p (g n) -> p g n", g=PHASE_PASSES)
-            for first in range(0, PHASE_PASSES, SCALE_DMA_PASSES):
-                g0 = phase * PHASE_PASSES + first
-                for q in range(8):
+            plane_i32 = planes[phase % 2][:].bitcast(I32)
+            g0 = phase * PHASE_PASSES
+            for low in range(8):
+                for q in (low, low + 8):
                     partition = 32 * (q // 4) + q % 4
                     nc.sync.dma_start(
-                        out=plane_i32[partition : P : 64, first : first + SCALE_DMA_PASSES, :],
-                        in_=w_scales_i32[g0 : g0 + SCALE_DMA_PASSES, q : 16 : 8, :].rearrange("g q n -> q g n"),
+                        out=plane_i32[partition : partition + 1, :].rearrange("o (g n) -> o g n", g=PHASE_PASSES),
+                        in_=w_scales_i32[g0 : g0 + PHASE_PASSES, q : q + 1, :].rearrange("g o n -> o g n"),
                     )
 
         def load_words_by_pass(phase):

@@ -40,7 +40,8 @@ PHASES = PASSES // PHASE_PASSES
 W_LOAD_PASSES = 2
 W_LOAD_BYTES = W_LOAD_PASSES * D_OUT * FP4_BYTES
 PHASE_LOADS = PHASE_PASSES // W_LOAD_PASSES
-assert PHASE_PASSES * BANK_COLS * FP4_BYTES == W_LOAD_BYTES
+TAIL_PASSES = 4
+TAIL_LOAD_BYTES = TAIL_PASSES * BANK_COLS * FP4_BYTES
 
 TWO_PI = 2.0 * math.pi
 TWO_PI_HIGH = 6.28125
@@ -62,7 +63,8 @@ def tile_attention_pa_k_kernel(tc, x, w_words, w_scales, out):
         grouped_pool = ctx.enter_context(tc.tile_pool(name="grouped", bufs=2))
         plane_pool = ctx.enter_context(tc.tile_pool(name="planes", bufs=1))
         word_pool = ctx.enter_context(tc.tile_pool(name="words", bufs=2 * PHASE_LOADS))
-        rot_pool = ctx.enter_context(tc.tile_pool(name="rotation", bufs=2))
+        tail_pool = ctx.enter_context(tc.tile_pool(name="tail_words", bufs=BANKS))
+        rot_pool = ctx.enter_context(tc.tile_pool(name="rotation", bufs=BANKS))
         acc_pool = ctx.enter_context(tc.psum_pool(name="acc", bufs=1))
         flip_pool = ctx.enter_context(tc.psum_pool(name="flipped", bufs=8 - BANKS))
         ctx.enter_context(tc.manual_schedule())
@@ -96,26 +98,25 @@ def tile_attention_pa_k_kernel(tc, x, w_words, w_scales, out):
                     )
 
         def load_words_by_pass(phase):
+            first = phase * PHASE_PASSES
             tiles = []
-            for i in range(PHASE_LOADS):
-                g0 = phase * PHASE_PASSES + i * W_LOAD_PASSES
+            for g0 in range(first, min(first + PHASE_PASSES, PASSES - TAIL_PASSES), W_LOAD_PASSES):
                 words = word_pool.tile([P, W_LOAD_BYTES], U8, name="words", align_bytes=64)
                 nc.sync.dma_start(
                     out=words[:].bitcast(I32).rearrange("p (g b) -> p g b", g=W_LOAD_PASSES),
                     in_=w_words_i32[g0 : g0 + W_LOAD_PASSES].rearrange("g p b -> p g b"),
                 )
-                tiles.append(words)
+                tiles.append((g0, words))
             return tiles
 
-        def load_words_by_bank(phase):
-            g0 = phase * PHASE_PASSES
+        def load_words_by_bank():
             bank_i32 = BANK_COLS * FP4_BYTES // 4
             tiles = []
             for j in range(BANKS):
-                words = word_pool.tile([P, W_LOAD_BYTES], U8, name="words", align_bytes=64)
+                words = tail_pool.tile([P, TAIL_LOAD_BYTES], U8, name="tail_words", align_bytes=64)
                 nc.sync.dma_start(
-                    out=words[:].bitcast(I32).rearrange("p (g b) -> p g b", g=PHASE_PASSES),
-                    in_=w_words_i32[g0 : g0 + PHASE_PASSES, :, j * bank_i32 : (j + 1) * bank_i32].rearrange(
+                    out=words[:].bitcast(I32).rearrange("p (g b) -> p g b", g=TAIL_PASSES),
+                    in_=w_words_i32[PASSES - TAIL_PASSES : PASSES, :, j * bank_i32 : (j + 1) * bank_i32].rearrange(
                         "g p b -> p g b"
                     ),
                 )
@@ -124,9 +125,7 @@ def tile_attention_pa_k_kernel(tc, x, w_words, w_scales, out):
 
         def load_phase(phase):
             load_scales(phase)
-            if phase < PHASES - 1:
-                return load_words_by_pass(phase)
-            return load_words_by_bank(phase)
+            return load_words_by_pass(phase)
 
         phase_words = {0: load_phase(0), 1: load_phase(1)}
 
@@ -229,26 +228,24 @@ def tile_attention_pa_k_kernel(tc, x, w_words, w_scales, out):
             )
             terms = products[:].rearrange("p s h (q t) -> p h q s t", t=2)
             rotated = rot_pool.tile([P, BANK_HEADS, PAIRS, 2], F32, name="rotated")
-            nc.vector.tensor_tensor(out=rotated[:], in0=terms[:, :, :, :, 0], in1=terms[:, :, :, :, 1], op=ALU.add)
+            adder = nc.gpsimd if j < BANKS - 1 else nc.vector
+            adder.tensor_tensor(out=rotated[:], in0=terms[:, :, :, :, 0], in1=terms[:, :, :, :, 1], op=ALU.add)
             nc.sync.dma_start(
                 out=out[j * BANK_HEADS : (j + 1) * BANK_HEADS].rearrange("h i d -> i h d"),
                 in_=rotated[:].rearrange("p h q s -> p h (q s)"),
             )
 
-        for phase in range(PHASES - 1):
-            for i, words in enumerate(phase_words[phase]):
+        for phase in range(PHASES):
+            for g0, words in phase_words[phase]:
                 for g in range(W_LOAD_PASSES):
                     for j in range(BANKS):
-                        multiply(
-                            phase * PHASE_PASSES + i * W_LOAD_PASSES + g,
-                            j,
-                            words,
-                            (g * D_OUT + j * BANK_COLS) * FP4_BYTES,
-                        )
+                        multiply(g0 + g, j, words, (g * D_OUT + j * BANK_COLS) * FP4_BYTES)
             if phase + 2 < PHASES:
                 phase_words[phase + 2] = load_phase(phase + 2)
+            if phase + 2 == PHASES - 1:
+                tail_words = load_words_by_bank()
 
-        for j, words in enumerate(phase_words[PHASES - 1]):
-            for g in range(PHASE_PASSES):
-                multiply((PHASES - 1) * PHASE_PASSES + g, j, words, g * BANK_COLS * FP4_BYTES)
+        for j, words in enumerate(tail_words):
+            for g in range(TAIL_PASSES):
+                multiply(PASSES - TAIL_PASSES + g, j, words, g * BANK_COLS * FP4_BYTES)
             rotate_and_store(j)

@@ -35,12 +35,14 @@ X_CHUNKS = PASSES // X_CHUNK_PASSES
 X_CHUNK_COLS = X_CHUNK_PASSES * K_PASS
 PASS_WORDS = K_PASS // 2
 
-PHASE_PASSES = 8
-PHASES = PASSES // PHASE_PASSES
+RUN_PASSES = 16
+RUNS = PASSES // RUN_PASSES
 W_LOAD_PASSES = 2
 W_LOAD_BYTES = W_LOAD_PASSES * D_OUT * FP4_BYTES
-PHASE_LOADS = PHASE_PASSES // W_LOAD_PASSES
+WORD_BUFS = 7
 TAIL_PASSES = 4
+W_LOADS = (PASSES - TAIL_PASSES) // W_LOAD_PASSES
+RUN_LOADS = RUN_PASSES // W_LOAD_PASSES
 TAIL_LOAD_BYTES = TAIL_PASSES * BANK_COLS * FP4_BYTES
 
 TWO_PI = 2.0 * math.pi
@@ -62,7 +64,7 @@ def tile_attention_pa_k_kernel(tc, x, w_words, w_scales, out):
         x_pool = ctx.enter_context(tc.tile_pool(name="x_raw", bufs=X_CHUNKS))
         grouped_pool = ctx.enter_context(tc.tile_pool(name="grouped", bufs=2))
         plane_pool = ctx.enter_context(tc.tile_pool(name="planes", bufs=1))
-        word_pool = ctx.enter_context(tc.tile_pool(name="words", bufs=2 * PHASE_LOADS))
+        word_pool = ctx.enter_context(tc.tile_pool(name="words", bufs=WORD_BUFS))
         tail_pool = ctx.enter_context(tc.tile_pool(name="tail_words", bufs=BANKS))
         rot_pool = ctx.enter_context(tc.tile_pool(name="rotation", bufs=BANKS))
         acc_pool = ctx.enter_context(tc.psum_pool(name="acc", bufs=1))
@@ -80,34 +82,30 @@ def tile_attention_pa_k_kernel(tc, x, w_words, w_scales, out):
         position_i32 = consts.tile([P, 1], I32, name="position_i32")
         nc.gpsimd.iota(position_i32[:], pattern=[[0, 1]], base=0, channel_multiplier=1)
 
-        planes = []
-        for i in range(2):
-            plane = plane_pool.tile([P, PHASE_PASSES * D_OUT], U8, name="planes%d" % i, align_bytes=64)
-            nc.vector.memset(plane[:].bitcast(I32), 0)
-            planes.append(plane)
+        planes = [
+            plane_pool.tile([P, RUN_PASSES * D_OUT], U8, name="planes%d" % i, align_bytes=64) for i in range(RUNS)
+        ]
+        nc.vector.memset(planes[0][:].bitcast(I32), 0)
 
-        def load_scales(phase):
-            plane_i32 = planes[phase % 2][:].bitcast(I32)
-            g0 = phase * PHASE_PASSES
+        def load_scales(run):
+            plane_i32 = planes[run][:].bitcast(I32)
+            g0 = run * RUN_PASSES
             for low in range(8):
                 for q in (low, low + 8):
                     partition = 32 * (q // 4) + q % 4
                     nc.sync.dma_start(
-                        out=plane_i32[partition : partition + 1, :].rearrange("o (g n) -> o g n", g=PHASE_PASSES),
-                        in_=w_scales_i32[g0 : g0 + PHASE_PASSES, q : q + 1, :].rearrange("g o n -> o g n"),
+                        out=plane_i32[partition : partition + 1, :].rearrange("o (g n) -> o g n", g=RUN_PASSES),
+                        in_=w_scales_i32[g0 : g0 + RUN_PASSES, q : q + 1, :].rearrange("g o n -> o g n"),
                     )
 
-        def load_words_by_pass(phase):
-            first = phase * PHASE_PASSES
-            tiles = []
-            for g0 in range(first, min(first + PHASE_PASSES, PASSES - TAIL_PASSES), W_LOAD_PASSES):
-                words = word_pool.tile([P, W_LOAD_BYTES], U8, name="words", align_bytes=64)
-                nc.sync.dma_start(
-                    out=words[:].bitcast(I32).rearrange("p (g b) -> p g b", g=W_LOAD_PASSES),
-                    in_=w_words_i32[g0 : g0 + W_LOAD_PASSES].rearrange("g p b -> p g b"),
-                )
-                tiles.append((g0, words))
-            return tiles
+        def load_words_by_pass(i):
+            g0 = i * W_LOAD_PASSES
+            words = word_pool.tile([P, W_LOAD_BYTES], U8, name="words", align_bytes=64)
+            nc.sync.dma_start(
+                out=words[:].bitcast(I32).rearrange("p (g b) -> p g b", g=W_LOAD_PASSES),
+                in_=w_words_i32[g0 : g0 + W_LOAD_PASSES].rearrange("g p b -> p g b"),
+            )
+            return words
 
         def load_words_by_bank():
             bank_i32 = BANK_COLS * FP4_BYTES // 4
@@ -123,11 +121,8 @@ def tile_attention_pa_k_kernel(tc, x, w_words, w_scales, out):
                 tiles.append(words)
             return tiles
 
-        def load_phase(phase):
-            load_scales(phase)
-            return load_words_by_pass(phase)
-
-        phase_words = {0: load_phase(0), 1: load_phase(1)}
+        load_scales(0)
+        loaded = [load_words_by_pass(i) for i in range(WORD_BUFS)]
 
         x_codes = consts.tile([P, PASSES * TOKENS], U32, name="x_codes", align_bytes=64)
         x_planes = consts.tile([P, PASSES * TOKENS], U8, name="x_planes", align_bytes=64)
@@ -157,6 +152,7 @@ def tile_attention_pa_k_kernel(tc, x, w_words, w_scales, out):
                 quantise_chunk(c - 1, waiting)
             waiting = grouped
         quantise_chunk(X_CHUNKS - 1, waiting)
+        nc.vector.memset(planes[1][:].bitcast(I32), 0)
 
         position = consts.tile([P, 1], F32, name="position")
         nc.vector.tensor_copy(out=position[:], in_=position_i32[:])
@@ -209,13 +205,13 @@ def tile_attention_pa_k_kernel(tc, x, w_words, w_scales, out):
         acc = [acc_pool.tile([P, BANK_COLS], F32, name="acc%d" % j) for j in range(BANKS)]
 
         def multiply(g, j, words, first_byte):
-            plane_col = (g % PHASE_PASSES) * D_OUT + j * BANK_COLS
+            plane_col = (g % RUN_PASSES) * D_OUT + j * BANK_COLS
             nc.tensor.matmul_mx(
                 out=acc[j][:],
                 lhsT=x_codes[:, g * TOKENS : (g + 1) * TOKENS].bitcast(FP8X4),
                 lhsT_scale=x_planes[:, g * TOKENS : (g + 1) * TOKENS],
                 rhs=words[:, first_byte : first_byte + BANK_COLS * FP4_BYTES].bitcast(FP4X4),
-                rhs_scale=planes[(g // PHASE_PASSES) % 2][:, plane_col : plane_col + BANK_COLS],
+                rhs_scale=planes[g // RUN_PASSES][:, plane_col : plane_col + BANK_COLS],
                 start=(g == 0),
                 stop=(g == PASSES - 1),
             )
@@ -235,14 +231,16 @@ def tile_attention_pa_k_kernel(tc, x, w_words, w_scales, out):
                 in_=rotated[:].rearrange("p h q s -> p h (q s)"),
             )
 
-        for phase in range(PHASES):
-            for g0, words in phase_words[phase]:
-                for g in range(W_LOAD_PASSES):
-                    for j in range(BANKS):
-                        multiply(g0 + g, j, words, (g * D_OUT + j * BANK_COLS) * FP4_BYTES)
-            if phase + 2 < PHASES:
-                phase_words[phase + 2] = load_phase(phase + 2)
-            if phase + 2 == PHASES - 1:
+        for i in range(W_LOADS):
+            for g in range(W_LOAD_PASSES):
+                for j in range(BANKS):
+                    multiply(i * W_LOAD_PASSES + g, j, loaded[i], (g * D_OUT + j * BANK_COLS) * FP4_BYTES)
+            following = i + WORD_BUFS
+            if following < W_LOADS:
+                loaded.append(load_words_by_pass(following))
+                if following == RUN_LOADS - 1:
+                    load_scales(1)
+            if following == W_LOADS - 1:
                 tail_words = load_words_by_bank()
 
         for j, words in enumerate(tail_words):

@@ -37,6 +37,7 @@ PASS_WORDS = K_PASS // 2
 
 RUN_PASSES = 16
 RUNS = PASSES // RUN_PASSES
+RUN_END_PASSES = 4
 W_LOAD_PASSES = 2
 W_LOAD_BYTES = W_LOAD_PASSES * D_OUT * FP4_BYTES
 WORD_BUFS = 7
@@ -89,13 +90,17 @@ def tile_attention_pa_k_kernel(tc, x, w_words, w_scales, out):
 
         def load_scales(run):
             plane_i32 = planes[run][:].bitcast(I32)
-            g0 = run * RUN_PASSES
-            for low in range(8):
-                for q in (low, low + 8):
+            row_i32 = D_OUT // 4
+            for first, last in ((0, RUN_PASSES - RUN_END_PASSES), (RUN_PASSES - RUN_END_PASSES, RUN_PASSES)):
+                for q in range(8):
                     partition = 32 * (q // 4) + q % 4
                     nc.sync.dma_start(
-                        out=plane_i32[partition : partition + 1, :].rearrange("o (g n) -> o g n", g=RUN_PASSES),
-                        in_=w_scales_i32[g0 : g0 + RUN_PASSES, q : q + 1, :].rearrange("g o n -> o g n"),
+                        out=plane_i32[partition : P : 64, first * row_i32 : last * row_i32].rearrange(
+                            "q (g n) -> q g n", g=last - first
+                        ),
+                        in_=w_scales_i32[run * RUN_PASSES + first : run * RUN_PASSES + last, q : 16 : 8, :].rearrange(
+                            "g q n -> q g n"
+                        ),
                     )
 
         def load_words_by_pass(i):

@@ -35,7 +35,7 @@ X_CHUNKS = PASSES // X_CHUNK_PASSES
 X_CHUNK_COLS = X_CHUNK_PASSES * K_PASS
 PASS_WORDS = K_PASS // 2
 
-RUN_PASSES = 16
+RUN_PASSES = 32
 RUNS = PASSES // RUN_PASSES
 RUN_END_PASSES = 4
 W_LOAD_PASSES = 2
@@ -43,7 +43,6 @@ W_LOAD_BYTES = W_LOAD_PASSES * D_OUT * FP4_BYTES
 WORD_BUFS = 7
 TAIL_PASSES = 4
 W_LOADS = (PASSES - TAIL_PASSES) // W_LOAD_PASSES
-RUN_LOADS = RUN_PASSES // W_LOAD_PASSES
 TAIL_LOAD_BYTES = TAIL_PASSES * BANK_COLS * FP4_BYTES
 
 TWO_PI = 2.0 * math.pi
@@ -157,7 +156,6 @@ def tile_attention_pa_k_kernel(tc, x, w_words, w_scales, out):
                 quantise_chunk(c - 1, waiting)
             waiting = grouped
         quantise_chunk(X_CHUNKS - 1, waiting)
-        nc.vector.memset(planes[1][:].bitcast(I32), 0)
 
         position = consts.tile([P, 1], F32, name="position")
         nc.vector.tensor_copy(out=position[:], in_=position_i32[:])
@@ -243,8 +241,6 @@ def tile_attention_pa_k_kernel(tc, x, w_words, w_scales, out):
             following = i + WORD_BUFS
             if following < W_LOADS:
                 loaded.append(load_words_by_pass(following))
-                if following == RUN_LOADS - 1:
-                    load_scales(1)
             if following == W_LOADS - 1:
                 tail_words = load_words_by_bank()
 

import math
from contextlib import ExitStack

import concourse.mybir as mybir
from concourse.masks import make_identity

F32 = mybir.dt.float32
BF16 = mybir.dt.bfloat16
I32 = mybir.dt.int32
U32 = mybir.dt.uint32
U8 = mybir.dt.uint8
FP8X4 = mybir.dt.float8_e4m3fn_x4
FP4X4 = mybir.dt.float4_e2m1fn_x4
ALU = mybir.AluOpType
ACT = mybir.ActivationFunctionType

P = 128
TOKENS = 128
D_IN = 16384
HEADS = 16
HEAD_DIM = 128
PAIRS = HEAD_DIM // 2
D_OUT = HEADS * HEAD_DIM
ROPE_BASE = 10000.0

K_PASS = 4 * P
PASSES = D_IN // K_PASS
BANK_COLS = 512
BANKS = D_OUT // BANK_COLS
BANK_HEADS = BANK_COLS // HEAD_DIM
FP4_BYTES = 2

X_CHUNK_PASSES = 8
X_CHUNKS = PASSES // X_CHUNK_PASSES
X_CHUNK_COLS = X_CHUNK_PASSES * K_PASS
PASS_WORDS = K_PASS // 2

RUN_PASSES = 32
RUNS = PASSES // RUN_PASSES
RUN_END_PASSES = 4
W_LOAD_PASSES = 2
W_LOAD_BYTES = W_LOAD_PASSES * D_OUT * FP4_BYTES
WORD_BUFS = 7
TAIL_PASSES = 4
W_LOADS = (PASSES - TAIL_PASSES) // W_LOAD_PASSES
TAIL_LOAD_BYTES = TAIL_PASSES * BANK_COLS * FP4_BYTES

TWO_PI = 2.0 * math.pi
TWO_PI_HIGH = 6.28125
TWO_PI_MID = round((TWO_PI - TWO_PI_HIGH) * 2.0**25) / 2.0**25
TWO_PI_LOW = TWO_PI - TWO_PI_HIGH - TWO_PI_MID
ROUNDER = 1.5 * 2.0**23

FLOPS = 2 * TOKENS * D_IN * D_OUT


def tile_attention_pa_k_kernel(tc, x, w_words, w_scales, out):
    nc = tc.nc
    w_words_i32 = w_words.bitcast(I32)
    w_scales_i32 = w_scales.bitcast(I32)

    with ExitStack() as ctx:
        consts = ctx.enter_context(tc.tile_pool(name="consts", bufs=1))
        x_pool = ctx.enter_context(tc.tile_pool(name="x_raw", bufs=X_CHUNKS))
        grouped_pool = ctx.enter_context(tc.tile_pool(name="grouped", bufs=2))
        plane_pool = ctx.enter_context(tc.tile_pool(name="planes", bufs=1))
        word_pool = ctx.enter_context(tc.tile_pool(name="words", bufs=WORD_BUFS))
        tail_pool = ctx.enter_context(tc.tile_pool(name="tail_words", bufs=BANKS))
        rot_pool = ctx.enter_context(tc.tile_pool(name="rotation", bufs=BANKS))
        acc_pool = ctx.enter_context(tc.psum_pool(name="acc", bufs=1))
        flip_pool = ctx.enter_context(tc.psum_pool(name="flipped", bufs=8 - BANKS))
        ctx.enter_context(tc.manual_schedule())

        x_raw = []
        for c in range(X_CHUNKS):
            chunk = x_pool.tile([P, X_CHUNK_COLS], BF16, name="x_raw")
            nc.sync.dma_start(out=chunk[:], in_=x[:, c * X_CHUNK_COLS : (c + 1) * X_CHUNK_COLS])
            x_raw.append(chunk)

        ident = consts.tile([P, P], F32, name="ident")
        make_identity(nc, ident[:])
        position_i32 = consts.tile([P, 1], I32, name="position_i32")
        nc.gpsimd.iota(position_i32[:], pattern=[[0, 1]], base=0, channel_multiplier=1)

        planes = [
            plane_pool.tile([P, RUN_PASSES * D_OUT], U8, name="planes%d" % i, align_bytes=64) for i in range(RUNS)
        ]
        nc.vector.memset(planes[0][:].bitcast(I32), 0)

        def load_scales(run):
            plane_i32 = planes[run][:].bitcast(I32)
            row_i32 = D_OUT // 4
            for first, last in ((0, RUN_PASSES - RUN_END_PASSES), (RUN_PASSES - RUN_END_PASSES, RUN_PASSES)):
                for q in range(8):
                    partition = 32 * (q // 4) + q % 4
                    nc.sync.dma_start(
                        out=plane_i32[partition : P : 64, first * row_i32 : last * row_i32].rearrange(
                            "q (g n) -> q g n", g=last - first
                        ),
                        in_=w_scales_i32[run * RUN_PASSES + first : run * RUN_PASSES + last, q : 16 : 8, :].rearrange(
                            "g q n -> q g n"
                        ),
                    )

        def load_words_by_pass(i):
            g0 = i * W_LOAD_PASSES
            words = word_pool.tile([P, W_LOAD_BYTES], U8, name="words", align_bytes=64)
            nc.sync.dma_start(
                out=words[:].bitcast(I32).rearrange("p (g b) -> p g b", g=W_LOAD_PASSES),
                in_=w_words_i32[g0 : g0 + W_LOAD_PASSES].rearrange("g p b -> p g b"),
            )
            return words

        def load_words_by_bank():
            bank_i32 = BANK_COLS * FP4_BYTES // 4
            tiles = []
            for j in range(BANKS):
                words = tail_pool.tile([P, TAIL_LOAD_BYTES], U8, name="tail_words", align_bytes=64)
                nc.sync.dma_start(
                    out=words[:].bitcast(I32).rearrange("p (g b) -> p g b", g=TAIL_PASSES),
                    in_=w_words_i32[PASSES - TAIL_PASSES : PASSES, :, j * bank_i32 : (j + 1) * bank_i32].rearrange(
                        "g p b -> p g b"
                    ),
                )
                tiles.append(words)
            return tiles

        load_scales(0)
        loaded = [load_words_by_pass(i) for i in range(WORD_BUFS)]

        x_codes = consts.tile([P, PASSES * TOKENS], U32, name="x_codes", align_bytes=64)
        x_planes = consts.tile([P, PASSES * TOKENS], U8, name="x_planes", align_bytes=64)

        def transpose_chunk(c):
            words = x_raw[c][:].bitcast(F32)
            grouped = grouped_pool.tile([P, X_CHUNK_COLS], BF16, name="grouped", align_bytes=64)
            grouped_words = grouped[:].bitcast(F32).rearrange("p (g r u) -> p g r u", g=X_CHUNK_PASSES, u=2)
            for b in range(X_CHUNK_PASSES // 2):
                flipped = flip_pool.tile([P, 2, 2, TOKENS], F32, name="flipped")
                for g in range(2):
                    first = (2 * b + g) * PASS_WORDS
                    for u in range(2):
                        nc.tensor.transpose(flipped[:, g, u, :], words[:, first + u : first + PASS_WORDS : 2], ident[:])
                copy = nc.vector.tensor_copy if b % 2 == 0 else nc.scalar.copy
                copy(out=grouped_words[:, 2 * b : 2 * b + 2], in_=flipped[:].rearrange("p g u r -> p g r u"))
            return grouped

        def quantise_chunk(c, grouped):
            cols = slice(c * X_CHUNK_PASSES * TOKENS, (c + 1) * X_CHUNK_PASSES * TOKENS)
            nc.vector.quantize_mx(out=x_codes[:, cols].bitcast(FP8X4), scales=x_planes[:, cols], in_=grouped[:])

        waiting = None
        for c in range(X_CHUNKS):
            grouped = transpose_chunk(c)
            if waiting is not None:
                quantise_chunk(c - 1, waiting)
            waiting = grouped
        quantise_chunk(X_CHUNKS - 1, waiting)

        position = consts.tile([P, 1], F32, name="position")
        nc.vector.tensor_copy(out=position[:], in_=position_i32[:])
        frequency = consts.tile([P, PAIRS], F32, name="frequency")
        nc.vector.memset(frequency[:, 0:1], 1.0)
        m = 1
        while m < PAIRS:
            nc.vector.tensor_scalar(
                out=frequency[:, m : 2 * m],
                in0=frequency[:, 0:m],
                scalar1=ROPE_BASE ** (-2.0 * m / HEAD_DIM),
                scalar2=None,
                op0=ALU.mult,
            )
            m *= 2
        angle = consts.tile([P, 2, PAIRS], F32, name="angle")
        nc.vector.tensor_scalar(
            out=angle[:, 0, :], in0=frequency[:], scalar1=position[:, 0:1], scalar2=None, op0=ALU.mult
        )
        nc.vector.tensor_scalar(
            out=angle[:, 1, :],
            in0=frequency[:],
            scalar1=position[:, 0:1],
            scalar2=0.5 * math.pi,
            op0=ALU.mult,
            op1=ALU.add,
        )
        shifted = consts.tile([P, 2, PAIRS], F32, name="shifted")
        nc.vector.tensor_scalar(
            out=shifted[:], in0=angle[:], scalar1=1.0 / TWO_PI, scalar2=ROUNDER, op0=ALU.mult, op1=ALU.add
        )
        turns = consts.tile([P, 2, PAIRS], F32, name="turns")
        nc.vector.tensor_scalar(out=turns[:], in0=shifted[:], scalar1=ROUNDER, scalar2=None, op0=ALU.subtract)
        reduced = angle
        for part, two_pi_part in enumerate((TWO_PI_HIGH, TWO_PI_MID, TWO_PI_LOW)):
            less = consts.tile([P, 2, PAIRS], F32, name="reduced%d" % part)
            nc.vector.scalar_tensor_tensor(
                out=less[:], in0=turns[:], scalar=-two_pi_part, in1=reduced[:], op0=ALU.mult, op1=ALU.add
            )
            reduced = less
        table = consts.tile([P, 2, PAIRS, 2], F32, name="table")
        nc.scalar.activation(out=table[:, 0, :, 0], in_=reduced[:, 1, :], func=ACT.Sin)
        nc.scalar.activation(out=table[:, 0, :, 1], in_=reduced[:, 0, :], func=ACT.Sin, scale=-1.0)
        nc.scalar.activation(out=table[:, 1, :, 0], in_=reduced[:, 0, :], func=ACT.Sin)
        nc.scalar.activation(out=table[:, 1, :, 1], in_=reduced[:, 1, :], func=ACT.Sin)
        table_by_head = (
            table[:].rearrange("p s q t -> p s (q t)").unsqueeze(2).to_broadcast([P, 2, BANK_HEADS, HEAD_DIM])
        )

        acc = [acc_pool.tile([P, BANK_COLS], F32, name="acc%d" % j) for j in range(BANKS)]

        def multiply(g, j, words, first_byte):
            plane_col = (g % RUN_PASSES) * D_OUT + j * BANK_COLS
            nc.tensor.matmul_mx(
                out=acc[j][:],
                lhsT=x_codes[:, g * TOKENS : (g + 1) * TOKENS].bitcast(FP8X4),
                lhsT_scale=x_planes[:, g * TOKENS : (g + 1) * TOKENS],
                rhs=words[:, first_byte : first_byte + BANK_COLS * FP4_BYTES].bitcast(FP4X4),
                rhs_scale=planes[g // RUN_PASSES][:, plane_col : plane_col + BANK_COLS],
                start=(g == 0),
                stop=(g == PASSES - 1),
            )

        def rotate_and_store(j):
            y = acc[j][:].rearrange("p (h d) -> p h d", h=BANK_HEADS).unsqueeze(1)
            products = rot_pool.tile([P, 2, BANK_HEADS, HEAD_DIM], F32, name="products")
            nc.vector.tensor_tensor(
                out=products[:], in0=y.to_broadcast([P, 2, BANK_HEADS, HEAD_DIM]), in1=table_by_head, op=ALU.mult
            )
            terms = products[:].rearrange("p s h (q t) -> p h q s t", t=2)
            rotated = rot_pool.tile([P, BANK_HEADS, PAIRS, 2], F32, name="rotated")
            adder = nc.gpsimd if j < BANKS - 1 else nc.vector
            adder.tensor_tensor(out=rotated[:], in0=terms[:, :, :, :, 0], in1=terms[:, :, :, :, 1], op=ALU.add)
            nc.sync.dma_start(
                out=out[j * BANK_HEADS : (j + 1) * BANK_HEADS].rearrange("h i d -> i h d"),
                in_=rotated[:].rearrange("p h q s -> p h (q s)"),
            )

        for i in range(W_LOADS):
            for g in range(W_LOAD_PASSES):
                for j in range(BANKS):
                    multiply(i * W_LOAD_PASSES + g, j, loaded[i], (g * D_OUT + j * BANK_COLS) * FP4_BYTES)
            following = i + WORD_BUFS
            if following < W_LOADS:
                loaded.append(load_words_by_pass(following))
            if following == W_LOADS - 1:
                tail_words = load_words_by_bank()

        for j, words in enumerate(tail_words):
            for g in range(TAIL_PASSES):
                multiply(PASSES - TAIL_PASSES + g, j, words, g * BANK_COLS * FP4_BYTES)
            rotate_and_store(j)
